import numpy as np
import ml_dtypes

BF16 = ml_dtypes.bfloat16


def bf(x):
    return np.asarray(x, np.float32).astype(BF16)


def f32(x):
    return np.asarray(x, np.float32)


def f64(x):
    return np.asarray(x).astype(np.float64)


def striped(idx):
    return np.tile(idx.reshape(-1, 16).T, (8, 1))


S, NBR, D, M, N, H, K = 1024, 4, 128, 256, 4096, 512, 8
G_END, CUTOFF = 5.5, 6.0
COEFF = -0.5 / (G_END / (D - 1)) ** 2


def sigmoid(v):
    return 1.0 / (1.0 + np.exp(-v))


def softplus(v):
    return np.log(1.0 + np.exp(v))


def setup_inputs():
    return {"h": bf(np.random.standard_normal((D, S))), "w_nbr": bf(np.random.standard_normal((D, M)) / np.sqrt(M)), "w_self": bf(np.random.standard_normal((D, M)) / np.sqrt(M)), "w_edge": bf(0.4 * np.random.standard_normal((D, M))), "b": f32(0.1 * np.random.standard_normal((M, 1))), "dist": f32(CUTOFF * np.random.uniform(size=(1, N))), "centres": f32(np.linspace(0.0, G_END, D).reshape(D, 1)), "offs": striped(np.concatenate([np.random.permutation(S)[:H] for _ in range(K)]))}


def reference(h, w_nbr, w_self, w_edge, b, dist, centres, offs):
    idx = offs[:16].T.reshape(-1)
    e = np.exp(COEFF * (f64(dist) - f64(centres)) ** 2)
    pre = f64(w_nbr).T @ f64(h)[:, idx] + np.repeat(f64(w_self).T @ f64(h), NBR, axis=1) + f64(w_edge).T @ e + f64(b)
    return e + sigmoid(pre[:D]) * softplus(pre[D:])

@@ -1,0 +1,113 @@
+import concourse.mybir as mybir
+
+F32 = mybir.dt.float32
+BF16 = mybir.dt.bfloat16
+U16 = mybir.dt.uint16
+FUNC = mybir.ActivationFunctionType
+
+P = 128
+ATOMS = 1024
+NEIGHBOURS = 4
+EDGES = ATOMS * NEIGHBOURS
+PIECE = 512
+PIECES = EDGES // PIECE
+PIECE_ATOMS = PIECE // NEIGHBOURS
+PIECE_OFFSET_COLUMNS = PIECE // 16
+COEFF = -0.5 / (5.5 / 127) ** 2
+EXP_CAP = 1.0e13
+
+FLOPS = 2 * 3 * P * (2 * P) * EDGES
+
+
+def tile_gnnff_kernel(tc, h, w_nbr, w_self, w_edge, b, dist, centres, offs, out):
+    nc = tc.nc
+    with (
+        tc.tile_pool(name="held", bufs=1) as held,
+        tc.tile_pool(name="work", bufs=3) as work,
+        tc.psum_pool(name="psum", bufs=1) as psum,
+    ):
+        offsets = held.tile([P, EDGES // 16], U16, name="offsets")
+        nc.sync.dma_start(offsets[:], offs)
+        feats = held.tile([P, ATOMS], BF16, name="feats")
+        nc.sync.dma_start(feats[:], h)
+        nbr_weights = held.tile([P, 2 * P], BF16, name="nbr_weights")
+        nc.sync.dma_start(nbr_weights[:], w_nbr)
+        self_weights = held.tile([P, 2 * P], BF16, name="self_weights")
+        nc.sync.dma_start(self_weights[:], w_self)
+        edge_weights = held.tile([P, 2 * P], BF16, name="edge_weights")
+        nc.sync.dma_start(edge_weights[:], w_edge)
+        filter_bias = held.tile([P, 1], F32, name="filter_bias")
+        nc.sync.dma_start(filter_bias[:], b[0:P, :])
+        core_bias = held.tile([P, 1], F32, name="core_bias")
+        nc.sync.dma_start(core_bias[:], b[P : 2 * P, :])
+
+        centre = held.tile([P, 1], F32, name="centre")
+        nc.scalar.dma_start(centre[:], centres)
+        lengths = held.tile([P, EDGES], F32, name="lengths")
+        for k in range(PIECES):
+            edges = slice(k * PIECE, (k + 1) * PIECE)
+            nc.scalar.dma_start(lengths[:, edges], dist[:, edges].to_broadcast([P, PIECE]))
+        minus_centre = held.tile([P, 1], F32, name="minus_centre")
+        nc.vector.tensor_scalar_mul(minus_centre[:], centre[:], -1.0)
+
+        scratch = held.tile([P, 1], F32, name="scratch")
+        nc.vector.memset(scratch[:], 0.0)
+        nc.scalar.activation(scratch[:], scratch[:], FUNC.Exp)
+
+        filter_rows = slice(0, P)
+        core_rows = slice(P, 2 * P)
+
+        def picked(k):
+            return feats[:].indirect(offsets[:, k * PIECE_OFFSET_COLUMNS : (k + 1) * PIECE_OFFSET_COLUMNS])
+
+        def own(k):
+            atoms = feats[:, k * PIECE_ATOMS : (k + 1) * PIECE_ATOMS]
+            return atoms.unsqueeze(2).to_broadcast([P, PIECE_ATOMS, NEIGHBOURS])
+
+        def by_atom(bank):
+            return bank.rearrange("p (a n) -> p a n", n=NEIGHBOURS)
+
+        core_pre = psum.tile([P, EDGES], F32, name="pre")
+
+        for k in range(PIECES):
+            edges = slice(k * PIECE, (k + 1) * PIECE)
+            nc.tensor.matmul(core_pre[:, edges], nbr_weights[:, core_rows], picked(k), start=True, stop=False)
+
+        gauss = held.tile([P, EDGES], F32, name="gauss")
+        gauss_bf16 = held.tile([P, EDGES], BF16, name="gauss_bf16")
+        for k in range(PIECES):
+            edges = slice(k * PIECE, (k + 1) * PIECE)
+            squares = work.tile([P, PIECE], F32, name="squares")
+            nc.scalar.activation(squares[:], lengths[:, edges], FUNC.Square, bias=minus_centre[:])
+            nc.scalar.activation(gauss[:, edges], squares[:], FUNC.Exp, scale=COEFF)
+            nc.vector.tensor_copy(gauss_bf16[:, edges], gauss[:, edges])
+
+        softplus = held.tile([P, EDGES], F32, name="softplus")
+        for k in range(PIECES):
+            edges = slice(k * PIECE, (k + 1) * PIECE)
+            nc.tensor.matmul(by_atom(core_pre[:, edges]), self_weights[:, core_rows], own(k), start=False, stop=False)
+            nc.tensor.matmul(core_pre[:, edges], edge_weights[:, core_rows], gauss_bf16[:, edges], start=False, stop=True)
+            core = work.tile([P, PIECE], F32, name="core")
+            nc.vector.tensor_scalar_add(core[:], core_pre[:, edges], core_bias[:])
+            grown = work.tile([P, PIECE], F32, name="grown")
+            nc.scalar.activation(grown[:], core[:], FUNC.Exp)
+            nc.vector.tensor_scalar_min(grown[:], grown[:], EXP_CAP)
+            log1p = work.tile([P, PIECE], F32, name="log1p")
+            nc.scalar.activation(log1p[:], grown[:], FUNC.Ln, bias=1.0)
+            nc.vector.tensor_max(softplus[:, edges], core[:], log1p[:])
+
+        filter_pre = psum.tile([P, EDGES], F32, name="pre")
+        for k in range(PIECES):
+            edges = slice(k * PIECE, (k + 1) * PIECE)
+            nc.tensor.matmul(by_atom(filter_pre[:, edges]), self_weights[:, filter_rows], own(k), start=True, stop=False)
+            nc.tensor.matmul(filter_pre[:, edges], edge_weights[:, filter_rows], gauss_bf16[:, edges], start=False, stop=False)
+
+        for k in range(PIECES):
+            edges = slice(k * PIECE, (k + 1) * PIECE)
+            nc.tensor.matmul(filter_pre[:, edges], nbr_weights[:, filter_rows], picked(k), start=False, stop=True)
+            gate = work.tile([P, PIECE], F32, name="gate")
+            nc.scalar.activation(gate[:], filter_pre[:, edges], FUNC.Sigmoid, bias=filter_bias[:])
+            result = work.tile([P, PIECE], F32, name="result")
+            nc.vector.tensor_mul(result[:], gate[:], softplus[:, edges])
+            nc.vector.tensor_add(result[:], result[:], gauss[:, edges])
+            nc.sync.dma_start(out[:, edges], result[:])

@@ -17,45 +17,52 @@ COEFF = -0.5 / (5.5 / 127) ** 2
 EXP_CAP = 1.0e13
 
 FLOPS = 2 * 3 * P * (2 * P) * EDGES
+WIDE = 2 * PIECE
+CORE_LAG = 7
 
 
 def tile_gnnff_kernel(tc, h, w_nbr, w_self, w_edge, b, dist, centres, offs, out):
     nc = tc.nc
     with (
         tc.tile_pool(name="held", bufs=1) as held,
+        tc.tile_pool(name="turn", bufs=1) as turn,
         tc.tile_pool(name="work", bufs=3) as work,
         tc.psum_pool(name="psum", bufs=1) as psum,
     ):
+        lengths = held.tile([P, EDGES], F32, name="lengths")
+
+        def load_lengths(queue, part):
+            edges = slice(part * WIDE, (part + 1) * WIDE)
+            queue.dma_start(lengths[:, edges], dist[:, edges].to_broadcast([P, WIDE]))
+
+        centre = held.tile([P, 1], F32, name="centre")
+        nc.scalar.dma_start(centre[:], centres)
+        load_lengths(nc.scalar, 0)
+        load_lengths(nc.scalar, 1)
         offsets = held.tile([P, EDGES // 16], U16, name="offsets")
         nc.sync.dma_start(offsets[:], offs)
         feats = held.tile([P, ATOMS], BF16, name="feats")
         nc.sync.dma_start(feats[:], h)
         nbr_weights = held.tile([P, 2 * P], BF16, name="nbr_weights")
         nc.sync.dma_start(nbr_weights[:], w_nbr)
+        load_lengths(nc.sync, 2)
+        load_lengths(nc.sync, 3)
         self_weights = held.tile([P, 2 * P], BF16, name="self_weights")
         nc.sync.dma_start(self_weights[:], w_self)
         edge_weights = held.tile([P, 2 * P], BF16, name="edge_weights")
         nc.sync.dma_start(edge_weights[:], w_edge)
-        filter_bias = held.tile([P, 1], F32, name="filter_bias")
-        nc.sync.dma_start(filter_bias[:], b[0:P, :])
         core_bias = held.tile([P, 1], F32, name="core_bias")
         nc.sync.dma_start(core_bias[:], b[P : 2 * P, :])
-
-        centre = held.tile([P, 1], F32, name="centre")
-        nc.scalar.dma_start(centre[:], centres)
-        lengths = held.tile([P, EDGES], F32, name="lengths")
-        for k in range(PIECES):
-            edges = slice(k * PIECE, (k + 1) * PIECE)
-            nc.scalar.dma_start(lengths[:, edges], dist[:, edges].to_broadcast([P, PIECE]))
+        filter_bias = held.tile([P, 1], F32, name="filter_bias")
+        nc.sync.dma_start(filter_bias[:], b[0:P, :])
         minus_centre = held.tile([P, 1], F32, name="minus_centre")
         nc.vector.tensor_scalar_mul(minus_centre[:], centre[:], -1.0)
 
-        scratch = held.tile([P, 1], F32, name="scratch")
-        nc.vector.memset(scratch[:], 0.0)
-        nc.scalar.activation(scratch[:], scratch[:], FUNC.Exp)
-
         filter_rows = slice(0, P)
         core_rows = slice(P, 2 * P)
+
+        def piece(k):
+            return slice(k * PIECE, (k + 1) * PIECE)
 
         def picked(k):
             return feats[:].indirect(offsets[:, k * PIECE_OFFSET_COLUMNS : (k + 1) * PIECE_OFFSET_COLUMNS])
@@ -70,44 +77,62 @@ def tile_gnnff_kernel(tc, h, w_nbr, w_self, w_edge, b, dist, centres, offs, out)
         core_pre = psum.tile([P, EDGES], F32, name="pre")
 
         for k in range(PIECES):
-            edges = slice(k * PIECE, (k + 1) * PIECE)
-            nc.tensor.matmul(core_pre[:, edges], nbr_weights[:, core_rows], picked(k), start=True, stop=False)
+            nc.tensor.matmul(core_pre[:, piece(k)], nbr_weights[:, core_rows], picked(k), start=True, stop=False)
 
+        squares = held.tile([P, EDGES], F32, name="squares")
         gauss = held.tile([P, EDGES], F32, name="gauss")
         gauss_bf16 = held.tile([P, EDGES], BF16, name="gauss_bf16")
-        for k in range(PIECES):
-            edges = slice(k * PIECE, (k + 1) * PIECE)
-            squares = work.tile([P, PIECE], F32, name="squares")
-            nc.scalar.activation(squares[:], lengths[:, edges], FUNC.Square, bias=minus_centre[:])
-            nc.scalar.activation(gauss[:, edges], squares[:], FUNC.Exp, scale=COEFF)
-            nc.vector.tensor_copy(gauss_bf16[:, edges], gauss[:, edges])
+        core = held.tile([P, EDGES], F32, name="core")
+        grown = turn.tile([P, EDGES], F32, name="grown_then_gate")
 
+        def square_stage(k):
+            if k % 2 == 0:
+                shifted = work.tile([P, PIECE], F32, name="shifted")
+                nc.vector.tensor_scalar_add(shifted[:], lengths[:, piece(k)], minus_centre[:])
+                nc.vector.tensor_mul(squares[:, piece(k)], shifted[:], shifted[:])
+            else:
+                nc.scalar.activation(squares[:, piece(k)], lengths[:, piece(k)], FUNC.Square, bias=minus_centre[:])
+
+        def gauss_stage(k):
+            nc.scalar.activation(gauss[:, piece(k)], squares[:, piece(k)], FUNC.Exp, scale=COEFF)
+
+        def round_stage(k):
+            nc.vector.tensor_copy(gauss_bf16[:, piece(k)], gauss[:, piece(k)])
+
+        def core_stage(k):
+            nc.tensor.matmul(by_atom(core_pre[:, piece(k)]), self_weights[:, core_rows], own(k), start=False, stop=False)
+            nc.tensor.matmul(core_pre[:, piece(k)], edge_weights[:, core_rows], gauss_bf16[:, piece(k)], start=False, stop=True)
+            nc.vector.tensor_scalar_add(core[:, piece(k)], core_pre[:, piece(k)], core_bias[:])
+            nc.scalar.activation(grown[:, piece(k)], core[:, piece(k)], FUNC.Exp)
+
+        for step in range(PIECES + CORE_LAG):
+            if step < PIECES:
+                square_stage(step)
+            if 1 <= step < PIECES + 1:
+                gauss_stage(step - 1)
+            if 2 <= step < PIECES + 2:
+                round_stage(step - 2)
+            if step >= CORE_LAG:
+                core_stage(step - CORE_LAG)
+
+        nc.vector.tensor_scalar_min(grown[:], grown[:], EXP_CAP)
+        log1p = held.tile([P, EDGES], F32, name="log1p")
         softplus = held.tile([P, EDGES], F32, name="softplus")
-        for k in range(PIECES):
-            edges = slice(k * PIECE, (k + 1) * PIECE)
-            nc.tensor.matmul(by_atom(core_pre[:, edges]), self_weights[:, core_rows], own(k), start=False, stop=False)
-            nc.tensor.matmul(core_pre[:, edges], edge_weights[:, core_rows], gauss_bf16[:, edges], start=False, stop=True)
-            core = work.tile([P, PIECE], F32, name="core")
-            nc.vector.tensor_scalar_add(core[:], core_pre[:, edges], core_bias[:])
-            grown = work.tile([P, PIECE], F32, name="grown")
-            nc.scalar.activation(grown[:], core[:], FUNC.Exp)
-            nc.vector.tensor_scalar_min(grown[:], grown[:], EXP_CAP)
-            log1p = work.tile([P, PIECE], F32, name="log1p")
-            nc.scalar.activation(log1p[:], grown[:], FUNC.Ln, bias=1.0)
-            nc.vector.tensor_max(softplus[:, edges], core[:], log1p[:])
+        for first in range(0, EDGES, WIDE):
+            edges = slice(first, first + WIDE)
+            nc.scalar.activation(log1p[:, edges], grown[:, edges], FUNC.Ln, bias=1.0)
+            nc.vector.tensor_max(softplus[:, edges], core[:, edges], log1p[:, edges])
 
         filter_pre = psum.tile([P, EDGES], F32, name="pre")
         for k in range(PIECES):
-            edges = slice(k * PIECE, (k + 1) * PIECE)
-            nc.tensor.matmul(by_atom(filter_pre[:, edges]), self_weights[:, filter_rows], own(k), start=True, stop=False)
-            nc.tensor.matmul(filter_pre[:, edges], edge_weights[:, filter_rows], gauss_bf16[:, edges], start=False, stop=False)
+            nc.tensor.matmul(by_atom(filter_pre[:, piece(k)]), self_weights[:, filter_rows], own(k), start=True, stop=False)
+            nc.tensor.matmul(filter_pre[:, piece(k)], edge_weights[:, filter_rows], gauss_bf16[:, piece(k)], start=False, stop=False)
 
+        gate = turn.tile([P, EDGES], F32, name="grown_then_gate")
+        result = held.tile([P, EDGES], F32, name="result")
         for k in range(PIECES):
-            edges = slice(k * PIECE, (k + 1) * PIECE)
-            nc.tensor.matmul(filter_pre[:, edges], nbr_weights[:, filter_rows], picked(k), start=False, stop=True)
-            gate = work.tile([P, PIECE], F32, name="gate")
-            nc.scalar.activation(gate[:], filter_pre[:, edges], FUNC.Sigmoid, bias=filter_bias[:])
-            result = work.tile([P, PIECE], F32, name="result")
-            nc.vector.tensor_mul(result[:], gate[:], softplus[:, edges])
-            nc.vector.tensor_add(result[:], result[:], gauss[:, edges])
-            nc.sync.dma_start(out[:, edges], result[:])
+            nc.tensor.matmul(filter_pre[:, piece(k)], nbr_weights[:, filter_rows], picked(k), start=False, stop=True)
+            nc.scalar.activation(gate[:, piece(k)], filter_pre[:, piece(k)], FUNC.Sigmoid, bias=filter_bias[:])
+            nc.vector.tensor_mul(result[:, piece(k)], gate[:, piece(k)], softplus[:, piece(k)])
+            nc.vector.tensor_add(result[:, piece(k)], result[:, piece(k)], gauss[:, piece(k)])
+            nc.sync.dma_start(out[:, piece(k)], result[:, piece(k)])

@@ -4,6 +4,7 @@ F32 = mybir.dt.float32
 BF16 = mybir.dt.bfloat16
 U16 = mybir.dt.uint16
 FUNC = mybir.ActivationFunctionType
+ALU = mybir.AluOpType
 
 P = 128
 ATOMS = 1024
@@ -18,7 +19,7 @@ EXP_CAP = 1.0e13
 
 FLOPS = 2 * 3 * P * (2 * P) * EDGES
 WIDE = 2 * PIECE
-CORE_LAG = 7
+HELD = 4
 
 
 def tile_gnnff_kernel(tc, h, w_nbr, w_self, w_edge, b, dist, centres, offs, out):
@@ -51,6 +52,8 @@ def tile_gnnff_kernel(tc, h, w_nbr, w_self, w_edge, b, dist, centres, offs, out)
         nc.sync.dma_start(self_weights[:], w_self)
         edge_weights = held.tile([P, 2 * P], BF16, name="edge_weights")
         nc.sync.dma_start(edge_weights[:], w_edge)
+        exp_bias = turn.tile([P, 1], F32, name="exp_bias_then_one")
+        nc.sync.dma_start(exp_bias[:], b[P : 2 * P, :])
         core_bias = held.tile([P, 1], F32, name="core_bias")
         nc.sync.dma_start(core_bias[:], b[P : 2 * P, :])
         filter_bias = held.tile([P, 1], F32, name="filter_bias")
@@ -74,19 +77,19 @@ def tile_gnnff_kernel(tc, h, w_nbr, w_self, w_edge, b, dist, centres, offs, out)
         def by_atom(bank):
             return bank.rearrange("p (a n) -> p a n", n=NEIGHBOURS)
 
-        core_pre = psum.tile([P, EDGES], F32, name="pre")
+        pre = psum.tile([P, EDGES], F32, name="pre")
 
         for k in range(PIECES):
-            nc.tensor.matmul(core_pre[:, piece(k)], nbr_weights[:, core_rows], picked(k), start=True, stop=False)
+            nc.tensor.matmul(pre[:, piece(k)], nbr_weights[:, core_rows], picked(k), start=True, stop=False)
 
         squares = held.tile([P, EDGES], F32, name="squares")
         gauss = held.tile([P, EDGES], F32, name="gauss")
         gauss_bf16 = held.tile([P, EDGES], BF16, name="gauss_bf16")
-        core = held.tile([P, EDGES], F32, name="core")
         grown = turn.tile([P, EDGES], F32, name="grown_then_gate")
+        core = held.tile([P, EDGES], F32, name="core")
 
         def square_stage(k):
-            if k % 2 == 0:
+            if k not in (0, 2):
                 shifted = work.tile([P, PIECE], F32, name="shifted")
                 nc.vector.tensor_scalar_add(shifted[:], lengths[:, piece(k)], minus_centre[:])
                 nc.vector.tensor_mul(squares[:, piece(k)], shifted[:], shifted[:])
@@ -99,40 +102,55 @@ def tile_gnnff_kernel(tc, h, w_nbr, w_self, w_edge, b, dist, centres, offs, out)
         def round_stage(k):
             nc.vector.tensor_copy(gauss_bf16[:, piece(k)], gauss[:, piece(k)])
 
+        def open_filter(k):
+            nc.tensor.matmul(by_atom(pre[:, piece(k)]), self_weights[:, filter_rows], own(k), start=True, stop=False)
+            nc.tensor.matmul(pre[:, piece(k)], edge_weights[:, filter_rows], gauss_bf16[:, piece(k)], start=False, stop=False)
+
         def core_stage(k):
-            nc.tensor.matmul(by_atom(core_pre[:, piece(k)]), self_weights[:, core_rows], own(k), start=False, stop=False)
-            nc.tensor.matmul(core_pre[:, piece(k)], edge_weights[:, core_rows], gauss_bf16[:, piece(k)], start=False, stop=True)
-            nc.vector.tensor_scalar_add(core[:, piece(k)], core_pre[:, piece(k)], core_bias[:])
-            nc.scalar.activation(grown[:, piece(k)], core[:, piece(k)], FUNC.Exp)
+            nc.tensor.matmul(by_atom(pre[:, piece(k)]), self_weights[:, core_rows], own(k), start=False, stop=False)
+            nc.tensor.matmul(pre[:, piece(k)], edge_weights[:, core_rows], gauss_bf16[:, piece(k)], start=False, stop=True)
+            nc.scalar.activation(grown[:, piece(k)], pre[:, piece(k)], FUNC.Exp, bias=exp_bias[:])
+            nc.vector.tensor_scalar_min(grown[:, piece(k)], grown[:, piece(k)], EXP_CAP)
+            if k >= HELD:
+                nc.vector.tensor_scalar_add(core[:, piece(k)], pre[:, piece(k)], core_bias[:])
 
-        for step in range(PIECES + CORE_LAG):
-            if step < PIECES:
-                square_stage(step)
-            if 1 <= step < PIECES + 1:
-                gauss_stage(step - 1)
-            if 2 <= step < PIECES + 2:
-                round_stage(step - 2)
-            if step >= CORE_LAG:
-                core_stage(step - CORE_LAG)
+        for k in range(PIECES + 1):
+            if k < PIECES:
+                square_stage(k)
+            if k >= 1:
+                gauss_stage(k - 1)
+        for k in range(PIECES):
+            round_stage(k)
+        for k in range(PIECES):
+            core_stage(k)
+        for k in range(HELD, PIECES):
+            open_filter(k)
 
-        nc.vector.tensor_scalar_min(grown[:], grown[:], EXP_CAP)
+        one = turn.tile([P, 1], F32, name="exp_bias_then_one")
+        nc.gpsimd.memset(one[:], 1.0)
+
+        log1p_held = turn.tile([P, HELD * PIECE], F32, name="log1p_then_weights")
         log1p = held.tile([P, EDGES], F32, name="log1p")
         softplus = held.tile([P, EDGES], F32, name="softplus")
-        for first in range(0, EDGES, WIDE):
-            edges = slice(first, first + WIDE)
-            nc.scalar.activation(log1p[:, edges], grown[:, edges], FUNC.Ln, bias=1.0)
-            nc.vector.tensor_max(softplus[:, edges], core[:, edges], log1p[:, edges])
+        for k in range(HELD):
+            nc.scalar.activation(log1p_held[:, piece(k)], grown[:, piece(k)], FUNC.Ln, bias=one[:])
+            nc.vector.scalar_tensor_tensor(
+                softplus[:, piece(k)], pre[:, piece(k)], core_bias[:], log1p_held[:, piece(k)], op0=ALU.add, op1=ALU.max
+            )
+            open_filter(k)
 
-        filter_pre = psum.tile([P, EDGES], F32, name="pre")
-        for k in range(PIECES):
-            nc.tensor.matmul(by_atom(filter_pre[:, piece(k)]), self_weights[:, filter_rows], own(k), start=True, stop=False)
-            nc.tensor.matmul(filter_pre[:, piece(k)], edge_weights[:, filter_rows], gauss_bf16[:, piece(k)], start=False, stop=False)
+        closing_weights = turn.tile([P, P], BF16, name="log1p_then_weights")
+        nc.vector.tensor_copy(closing_weights[:], nbr_weights[:, filter_rows])
+
+        for k in range(HELD, PIECES):
+            nc.scalar.activation(log1p[:, piece(k)], grown[:, piece(k)], FUNC.Ln, bias=one[:])
+            nc.vector.tensor_max(softplus[:, piece(k)], core[:, piece(k)], log1p[:, piece(k)])
 
         gate = turn.tile([P, EDGES], F32, name="grown_then_gate")
         result = held.tile([P, EDGES], F32, name="result")
         for k in range(PIECES):
-            nc.tensor.matmul(filter_pre[:, piece(k)], nbr_weights[:, filter_rows], picked(k), start=False, stop=True)
-            nc.scalar.activation(gate[:, piece(k)], filter_pre[:, piece(k)], FUNC.Sigmoid, bias=filter_bias[:])
+            nc.tensor.matmul(pre[:, piece(k)], closing_weights[:], picked(k), start=False, stop=True)
+            nc.scalar.activation(gate[:, piece(k)], pre[:, piece(k)], FUNC.Sigmoid, bias=filter_bias[:])
             nc.vector.tensor_mul(result[:, piece(k)], gate[:, piece(k)], softplus[:, piece(k)])
             nc.vector.tensor_add(result[:, piece(k)], result[:, piece(k)], gauss[:, piece(k)])
             nc.sync.dma_start(out[:, piece(k)], result[:, piece(k)])

@@ -52,9 +52,9 @@ def tile_gnnff_kernel(tc, h, w_nbr, w_self, w_edge, b, dist, centres, offs, out)
         nc.sync.dma_start(self_weights[:], w_self)
         edge_weights = held.tile([P, 2 * P], BF16, name="edge_weights")
         nc.sync.dma_start(edge_weights[:], w_edge)
-        exp_bias = turn.tile([P, 1], F32, name="exp_bias_then_one")
+        exp_bias = turn.tile([P, 1], F32, name="exp_bias_then_log1p")
         nc.sync.dma_start(exp_bias[:], b[P : 2 * P, :])
-        core_bias = held.tile([P, 1], F32, name="core_bias")
+        core_bias = turn.tile([P, 1], F32, name="core_bias_then_weights")
         nc.sync.dma_start(core_bias[:], b[P : 2 * P, :])
         filter_bias = held.tile([P, 1], F32, name="filter_bias")
         nc.sync.dma_start(filter_bias[:], b[0:P, :])
@@ -126,24 +126,20 @@ def tile_gnnff_kernel(tc, h, w_nbr, w_self, w_edge, b, dist, centres, offs, out)
         for k in range(HELD, PIECES):
             open_filter(k)
 
-        one = turn.tile([P, 1], F32, name="exp_bias_then_one")
-        nc.gpsimd.memset(one[:], 1.0)
-
-        log1p_held = turn.tile([P, HELD * PIECE], F32, name="log1p_then_weights")
-        log1p = held.tile([P, EDGES], F32, name="log1p")
+        log1p = turn.tile([P, EDGES], F32, name="exp_bias_then_log1p")
         softplus = held.tile([P, EDGES], F32, name="softplus")
         for k in range(HELD):
-            nc.scalar.activation(log1p_held[:, piece(k)], grown[:, piece(k)], FUNC.Ln, bias=one[:])
+            nc.scalar.activation(log1p[:, piece(k)], grown[:, piece(k)], FUNC.Ln, bias=1.0)
             nc.vector.scalar_tensor_tensor(
-                softplus[:, piece(k)], pre[:, piece(k)], core_bias[:], log1p_held[:, piece(k)], op0=ALU.add, op1=ALU.max
+                softplus[:, piece(k)], pre[:, piece(k)], core_bias[:], log1p[:, piece(k)], op0=ALU.add, op1=ALU.max
             )
             open_filter(k)
 
-        closing_weights = turn.tile([P, P], BF16, name="log1p_then_weights")
+        closing_weights = turn.tile([P, P], BF16, name="core_bias_then_weights")
         nc.vector.tensor_copy(closing_weights[:], nbr_weights[:, filter_rows])
 
         for k in range(HELD, PIECES):
-            nc.scalar.activation(log1p[:, piece(k)], grown[:, piece(k)], FUNC.Ln, bias=one[:])
+            nc.scalar.activation(log1p[:, piece(k)], grown[:, piece(k)], FUNC.Ln, bias=1.0)
             nc.vector.tensor_max(softplus[:, piece(k)], core[:, piece(k)], log1p[:, piece(k)])
 
         gate = turn.tile([P, EDGES], F32, name="grown_then_gate")

@@ -39,13 +39,13 @@ def tile_gnnff_kernel(tc, h, w_nbr, w_self, w_edge, b, dist, centres, offs, out)
         centre = held.tile([P, 1], F32, name="centre")
         nc.scalar.dma_start(centre[:], centres)
         load_lengths(nc.scalar, 0)
-        load_lengths(nc.scalar, 1)
         offsets = held.tile([P, EDGES // 16], U16, name="offsets")
         nc.sync.dma_start(offsets[:], offs)
         feats = held.tile([P, ATOMS], BF16, name="feats")
         nc.sync.dma_start(feats[:], h)
         nbr_weights = held.tile([P, 2 * P], BF16, name="nbr_weights")
         nc.sync.dma_start(nbr_weights[:], w_nbr)
+        load_lengths(nc.sync, 1)
         load_lengths(nc.sync, 2)
         load_lengths(nc.sync, 3)
         self_weights = held.tile([P, 2 * P], BF16, name="self_weights")

@@ -39,6 +39,9 @@ def tile_gnnff_kernel(tc, h, w_nbr, w_self, w_edge, b, dist, centres, offs, out)
         centre = held.tile([P, 1], F32, name="centre")
         nc.scalar.dma_start(centre[:], centres)
         load_lengths(nc.scalar, 0)
+        warm = held.tile([P, 1], F32, name="warm")
+        nc.vector.memset(warm[:], 0.0)
+        nc.scalar.activation(warm[:], warm[:], FUNC.Exp)
         offsets = held.tile([P, EDGES // 16], U16, name="offsets")
         nc.sync.dma_start(offsets[:], offs)
         feats = held.tile([P, ATOMS], BF16, name="feats")

@@ -61,8 +61,6 @@ def tile_gnnff_kernel(tc, h, w_nbr, w_self, w_edge, b, dist, centres, offs, out)
         nc.sync.dma_start(core_bias[:], b[P : 2 * P, :])
         filter_bias = held.tile([P, 1], F32, name="filter_bias")
         nc.sync.dma_start(filter_bias[:], b[0:P, :])
-        minus_centre = held.tile([P, 1], F32, name="minus_centre")
-        nc.vector.tensor_scalar_mul(minus_centre[:], centre[:], -1.0)
 
         filter_rows = slice(0, P)
         core_rows = slice(P, 2 * P)
@@ -94,10 +92,10 @@ def tile_gnnff_kernel(tc, h, w_nbr, w_self, w_edge, b, dist, centres, offs, out)
         def square_stage(k):
             if k not in (0, 2):
                 shifted = work.tile([P, PIECE], F32, name="shifted")
-                nc.vector.tensor_scalar_add(shifted[:], lengths[:, piece(k)], minus_centre[:])
+                nc.vector.tensor_scalar_sub(shifted[:], lengths[:, piece(k)], centre[:])
                 nc.vector.tensor_mul(squares[:, piece(k)], shifted[:], shifted[:])
             else:
-                nc.scalar.activation(squares[:, piece(k)], lengths[:, piece(k)], FUNC.Square, bias=minus_centre[:])
+                nc.scalar.activation(squares[:, piece(k)], lengths[:, piece(k)], FUNC.Square, bias=centre[:], scale=-1.0)
 
         def gauss_stage(k):
             nc.scalar.activation(gauss[:, piece(k)], squares[:, piece(k)], FUNC.Exp, scale=COEFF)

@@ -19,7 +19,7 @@ EXP_CAP = 1.0e13
 
 FLOPS = 2 * 3 * P * (2 * P) * EDGES
 WIDE = 2 * PIECE
-HELD = 4
+HELD = 2
 
 
 def tile_gnnff_kernel(tc, h, w_nbr, w_self, w_edge, b, dist, centres, offs, out):

import concourse.mybir as mybir

F32 = mybir.dt.float32
BF16 = mybir.dt.bfloat16
U16 = mybir.dt.uint16
FUNC = mybir.ActivationFunctionType
ALU = mybir.AluOpType

P = 128
ATOMS = 1024
NEIGHBOURS = 4
EDGES = ATOMS * NEIGHBOURS
PIECE = 512
PIECES = EDGES // PIECE
PIECE_ATOMS = PIECE // NEIGHBOURS
PIECE_OFFSET_COLUMNS = PIECE // 16
COEFF = -0.5 / (5.5 / 127) ** 2
EXP_CAP = 1.0e13

FLOPS = 2 * 3 * P * (2 * P) * EDGES
WIDE = 2 * PIECE
HELD = 2


def tile_gnnff_kernel(tc, h, w_nbr, w_self, w_edge, b, dist, centres, offs, out):
    nc = tc.nc
    with (
        tc.tile_pool(name="held", bufs=1) as held,
        tc.tile_pool(name="turn", bufs=1) as turn,
        tc.tile_pool(name="work", bufs=3) as work,
        tc.psum_pool(name="psum", bufs=1) as psum,
    ):
        lengths = held.tile([P, EDGES], F32, name="lengths")

        def load_lengths(queue, part):
            edges = slice(part * WIDE, (part + 1) * WIDE)
            queue.dma_start(lengths[:, edges], dist[:, edges].to_broadcast([P, WIDE]))

        centre = held.tile([P, 1], F32, name="centre")
        nc.scalar.dma_start(centre[:], centres)
        load_lengths(nc.scalar, 0)
        warm = held.tile([P, 1], F32, name="warm")
        nc.vector.memset(warm[:], 0.0)
        nc.scalar.activation(warm[:], warm[:], FUNC.Exp)
        offsets = held.tile([P, EDGES // 16], U16, name="offsets")
        nc.sync.dma_start(offsets[:], offs)
        feats = held.tile([P, ATOMS], BF16, name="feats")
        nc.sync.dma_start(feats[:], h)
        nbr_weights = held.tile([P, 2 * P], BF16, name="nbr_weights")
        nc.sync.dma_start(nbr_weights[:], w_nbr)
        load_lengths(nc.sync, 1)
        load_lengths(nc.sync, 2)
        load_lengths(nc.sync, 3)
        self_weights = held.tile([P, 2 * P], BF16, name="self_weights")
        nc.sync.dma_start(self_weights[:], w_self)
        edge_weights = held.tile([P, 2 * P], BF16, name="edge_weights")
        nc.sync.dma_start(edge_weights[:], w_edge)
        exp_bias = turn.tile([P, 1], F32, name="exp_bias_then_log1p")
        nc.sync.dma_start(exp_bias[:], b[P : 2 * P, :])
        core_bias = turn.tile([P, 1], F32, name="core_bias_then_weights")
        nc.sync.dma_start(core_bias[:], b[P : 2 * P, :])
        filter_bias = held.tile([P, 1], F32, name="filter_bias")
        nc.sync.dma_start(filter_bias[:], b[0:P, :])

        filter_rows = slice(0, P)
        core_rows = slice(P, 2 * P)

        def piece(k):
            return slice(k * PIECE, (k + 1) * PIECE)

        def picked(k):
            return feats[:].indirect(offsets[:, k * PIECE_OFFSET_COLUMNS : (k + 1) * PIECE_OFFSET_COLUMNS])

        def own(k):
            atoms = feats[:, k * PIECE_ATOMS : (k + 1) * PIECE_ATOMS]
            return atoms.unsqueeze(2).to_broadcast([P, PIECE_ATOMS, NEIGHBOURS])

        def by_atom(bank):
            return bank.rearrange("p (a n) -> p a n", n=NEIGHBOURS)

        pre = psum.tile([P, EDGES], F32, name="pre")

        for k in range(PIECES):
            nc.tensor.matmul(pre[:, piece(k)], nbr_weights[:, core_rows], picked(k), start=True, stop=False)

        squares = held.tile([P, EDGES], F32, name="squares")
        gauss = held.tile([P, EDGES], F32, name="gauss")
        gauss_bf16 = held.tile([P, EDGES], BF16, name="gauss_bf16")
        grown = turn.tile([P, EDGES], F32, name="grown_then_gate")
        core = held.tile([P, EDGES], F32, name="core")

        def square_stage(k):
            if k not in (0, 2):
                shifted = work.tile([P, PIECE], F32, name="shifted")
                nc.vector.tensor_scalar_sub(shifted[:], lengths[:, piece(k)], centre[:])
                nc.vector.tensor_mul(squares[:, piece(k)], shifted[:], shifted[:])
            else:
                nc.scalar.activation(squares[:, piece(k)], lengths[:, piece(k)], FUNC.Square, bias=centre[:], scale=-1.0)

        def gauss_stage(k):
            nc.scalar.activation(gauss[:, piece(k)], squares[:, piece(k)], FUNC.Exp, scale=COEFF)

        def round_stage(k):
            nc.vector.tensor_copy(gauss_bf16[:, piece(k)], gauss[:, piece(k)])

        def open_filter(k):
            nc.tensor.matmul(by_atom(pre[:, piece(k)]), self_weights[:, filter_rows], own(k), start=True, stop=False)
            nc.tensor.matmul(pre[:, piece(k)], edge_weights[:, filter_rows], gauss_bf16[:, piece(k)], start=False, stop=False)

        def core_stage(k):
            nc.tensor.matmul(by_atom(pre[:, piece(k)]), self_weights[:, core_rows], own(k), start=False, stop=False)
            nc.tensor.matmul(pre[:, piece(k)], edge_weights[:, core_rows], gauss_bf16[:, piece(k)], start=False, stop=True)
            nc.scalar.activation(grown[:, piece(k)], pre[:, piece(k)], FUNC.Exp, bias=exp_bias[:])
            nc.vector.tensor_scalar_min(grown[:, piece(k)], grown[:, piece(k)], EXP_CAP)
            if k >= HELD:
                nc.vector.tensor_scalar_add(core[:, piece(k)], pre[:, piece(k)], core_bias[:])

        for k in range(PIECES + 1):
            if k < PIECES:
                square_stage(k)
            if k >= 1:
                gauss_stage(k - 1)
        for k in range(PIECES):
            round_stage(k)
        for k in range(PIECES):
            core_stage(k)
        for k in range(HELD, PIECES):
            open_filter(k)

        log1p = turn.tile([P, EDGES], F32, name="exp_bias_then_log1p")
        softplus = held.tile([P, EDGES], F32, name="softplus")
        for k in range(HELD):
            nc.scalar.activation(log1p[:, piece(k)], grown[:, piece(k)], FUNC.Ln, bias=1.0)
            nc.vector.scalar_tensor_tensor(
                softplus[:, piece(k)], pre[:, piece(k)], core_bias[:], log1p[:, piece(k)], op0=ALU.add, op1=ALU.max
            )
            open_filter(k)

        closing_weights = turn.tile([P, P], BF16, name="core_bias_then_weights")
        nc.vector.tensor_copy(closing_weights[:], nbr_weights[:, filter_rows])

        for k in range(HELD, PIECES):
            nc.scalar.activation(log1p[:, piece(k)], grown[:, piece(k)], FUNC.Ln, bias=1.0)
            nc.vector.tensor_max(softplus[:, piece(k)], core[:, piece(k)], log1p[:, piece(k)])

        gate = turn.tile([P, EDGES], F32, name="grown_then_gate")
        result = held.tile([P, EDGES], F32, name="result")
        for k in range(PIECES):
            nc.tensor.matmul(pre[:, piece(k)], closing_weights[:], picked(k), start=False, stop=True)
            nc.scalar.activation(gate[:, piece(k)], pre[:, piece(k)], FUNC.Sigmoid, bias=filter_bias[:])
            nc.vector.tensor_mul(result[:, piece(k)], gate[:, piece(k)], softplus[:, piece(k)])
            nc.vector.tensor_add(result[:, piece(k)], result[:, piece(k)], gauss[:, piece(k)])
            nc.sync.dma_start(out[:, piece(k)], result[:, piece(k)])
